import numpy as np
import ml_dtypes


def mxq(x, axis, fmt="e4m3"):
    dtype, down = {"e4m3": (ml_dtypes.float8_e4m3fn, 7), "e5m2": (ml_dtypes.float8_e5m2, 14)}[fmt]
    v = np.moveaxis(np.asarray(x, np.float32).astype(ml_dtypes.bfloat16).astype(np.float64), axis, -1)
    blocks = v.reshape(v.shape[:-1] + (-1, 32))
    amax = np.abs(blocks).max(-1, keepdims=True)
    byte = np.maximum(np.where(amax > 0, np.frexp(amax)[1] - 1 + 127, 0) - down, 1)
    scale = np.exp2(byte - 127.0)
    codes = (blocks / scale).astype(np.float32).astype(dtype).astype(np.float64)
    return np.moveaxis((codes * scale).reshape(v.shape), -1, axis)


WIDE = False


def mx_kscale(k):
    if not WIDE:
        return np.ones(k)
    levels = np.array([10, -10, 5, -5, 0])
    a = np.random.permutation(np.resize(levels, k // 512 * 4)).reshape(k // 512, 4)
    idx = np.arange(k)
    return np.exp2(a[idx // 512, idx % 128 // 32])


BF16 = ml_dtypes.bfloat16


def bf(x):
    return np.asarray(x, np.float32).astype(BF16)


def f64(x):
    return np.asarray(x).astype(np.float64)


E2M1 = np.array([0.0, 0.5, 1.0, 1.5, 2.0, 3.0, 4.0, 6.0, -0.0, -0.5, -1.0, -1.5, -2.0, -3.0, -4.0, -6.0])


def pack_weight(w, fmt):
    k, n = w.shape
    w = f64(bf(w)).reshape(k // 32, 32, n)
    amax = np.abs(w).max(1)
    if fmt == "e4m3":
        byte = np.frexp(amax)[1] - 1 + 127 - 7
    else:
        mant, ex = np.frexp(amax / 6.0)
        byte = np.where(mant > 0.5, ex, ex - 1) + 127
    byte = np.clip(np.where(amax > 0, byte, 1), 1, 254)
    scaled = (w * np.exp2(127.0 - byte)[:, None, :]).reshape(k, n).astype(np.float32)
    by_word = np.ascontiguousarray(scaled.reshape(k // 512, 128, 4, n).transpose(0, 1, 3, 2))
    if fmt == "e4m3":
        words = by_word.astype(ml_dtypes.float8_e4m3fn).view(np.uint8)
    else:
        c = by_word.astype(ml_dtypes.float4_e2m1fn).view(np.uint8) & 0xF
        words = c[..., 0::2] | (c[..., 1::2] << 4)
    return np.ascontiguousarray(words), np.ascontiguousarray(byte.astype(np.uint8).reshape(k // 512, 16, n))


def unpack_weight(words, scales, fmt):
    g, p, n, _ = words.shape
    if fmt == "e4m3":
        vals = np.ascontiguousarray(words).view(ml_dtypes.float8_e4m3fn).astype(np.float64)
    else:
        nib = np.empty((g, p, n, 4), np.uint8)
        nib[..., 0::2] = words & 0xF
        nib[..., 1::2] = words >> 4
        vals = E2M1[nib]
    vals = vals * np.repeat(np.exp2(scales.astype(np.float64) - 127.0), 8, axis=1)[..., None]
    return vals.transpose(0, 1, 3, 2).reshape(g * 512, n)

def pack4(w):
    words, scales = pack_weight(w, "e2m1")
    return words.reshape(words.shape[0], 128, -1), scales


def unpack4(words, scales):
    return unpack_weight(words.reshape(words.shape[0], 128, -1, 2), scales, "e2m1")


B, C, H, W, RQ, RV = 1, 2048, 64, 32, 8, 2
DQ, DV = C // RQ, C // RV
N = H * W


def maxpool2(x):
    b, c, h, w = x.shape
    return x.reshape(b, c, h // 2, 2, w // 2, 2).max(axis=(3, 5))


def setup_inputs():
    s = mx_kscale(C)
    imgs = bf(np.random.standard_normal((B, C, H, W)) * s[None, :, None, None])
    w_kv = np.random.standard_normal((DQ + DV, C)) * 0.5 / np.sqrt(C) / s[None, :]
    words, scales = pack4(np.ascontiguousarray(w_kv.T))
    return {"imgs": imgs, "w_kv_words": words, "w_kv_scales": scales}


def reference(imgs, w_kv_words, w_kv_scales):
    x = f64(imgs).reshape(B, C, N)
    kv = (unpack4(w_kv_words, w_kv_scales).T @ mxq(x, 1, "e4m3")).reshape(B, DQ + DV, H, W)
    return maxpool2(kv[:, :DQ]), maxpool2(kv[:, DQ:])

@@ -1,0 +1,145 @@
+from contextlib import ExitStack
+
+import concourse.mybir as mybir
+
+BF16 = mybir.dt.bfloat16
+F32 = mybir.dt.float32
+I32 = mybir.dt.int32
+U32 = mybir.dt.uint32
+U8 = mybir.dt.uint8
+FP8X4 = mybir.dt.float8_e4m3fn_x4
+FP4X4 = mybir.dt.float4_e2m1fn_x4
+
+P = 128
+PACK = 4
+K_PASS = P * PACK
+CHANNELS = 2048
+IMAGE_ROWS = 64
+IMAGE_COLS = 32
+PIXELS = IMAGE_ROWS * IMAGE_COLS
+KEY_ROWS = 256
+VALUE_ROWS = 1024
+OUT_ROWS = KEY_ROWS + VALUE_ROWS
+PASSES = CHANNELS // K_PASS
+ROW_TILES = OUT_ROWS // P
+N_TILE = 512
+COLUMN_TILES = PIXELS // N_TILE
+TILE_IMAGE_ROWS = N_TILE // IMAGE_COLS
+POOLED = N_TILE // 4
+PSUM_BANKS = 8
+GROUP = 5
+HEAD_VECTOR_COLS = 352
+
+FLOPS = 2 * OUT_ROWS * CHANNELS * PIXELS
+
+
+def tile_selfattentionconv2d_pa_kernel(tc, imgs, w_kv_words, w_kv_scales, out_0, out_1):
+    nc = tc.nc
+
+    x = imgs.rearrange("b (g p j) h w -> (b g) p j (h w)", p=P, j=PACK)
+    key_blocks = out_0.rearrange("b (m p) i j -> (b m) p (i j)", p=P)
+    value_blocks = out_1.rearrange("b (m p) i j -> (b m) p (i j)", p=P)
+    out_blocks = [key_blocks[m] for m in range(KEY_ROWS // P)]
+    out_blocks.extend([value_blocks[m] for m in range(VALUE_ROWS // P)])
+
+    with ExitStack() as ctx:
+        keep = ctx.enter_context(tc.tile_pool(name="keep", bufs=1))
+        raw_pool = ctx.enter_context(tc.tile_pool(name="raw", bufs=PASSES * COLUMN_TILES))
+        grouped_pool = ctx.enter_context(tc.tile_pool(name="grouped", bufs=4))
+        mx_pool = ctx.enter_context(tc.tile_pool(name="mx", bufs=PASSES * COLUMN_TILES))
+        pooled_pool = ctx.enter_context(tc.tile_pool(name="pooled", bufs=2 * GROUP))
+        psum = ctx.enter_context(tc.psum_pool(name="psum", bufs=PSUM_BANKS))
+
+        w_words = keep.tile([P, PASSES, 2 * OUT_ROWS], U8, align_bytes=64)
+        w_planes = keep.tile([P, PASSES, OUT_ROWS], U8, align_bytes=64)
+        nc.vector.memset(w_planes[:].bitcast(I32), 0)
+
+        raw = {}
+
+        def load_chunk(t, g):
+            raw[t, g] = raw_pool.tile([P, PACK, N_TILE], BF16, name="raw")
+            nc.sync.dma_start(out=raw[t, g][:], in_=x[g][:, :, t * N_TILE : (t + 1) * N_TILE])
+
+        def load_scales():
+            rows = w_kv_scales.rearrange("g q n -> q g n")
+            for b in range(2):
+                for r in range(4):
+                    nc.sync.dma_start(
+                        out=w_planes[32 * b + r : P : 64].bitcast(I32),
+                        in_=rows[4 * b + r : 16 : 8].bitcast(I32),
+                    )
+
+        def load_words(g):
+            nc.sync.dma_start(out=w_words[:, g, :].bitcast(I32), in_=w_kv_words[g].bitcast(I32))
+
+        load_chunk(0, 0)
+        load_scales()
+        load_words(0)
+        for g in range(1, PASSES):
+            load_chunk(0, g)
+            load_words(g)
+        for t in range(1, COLUMN_TILES):
+            for g in range(PASSES):
+                load_chunk(t, g)
+
+        x_codes = {}
+        x_planes = {}
+
+        def regroup(engine_copy, grouped, chunk, first, last):
+            engine_copy(
+                out=grouped[:, first:last, :].rearrange("p (c i) j -> p c j i", i=4),
+                in_=chunk[:, :, first:last].rearrange("p j (c i) -> p c j i", i=4),
+            )
+
+        def quantise_chunk(t, g):
+            grouped = grouped_pool.tile([P, N_TILE, PACK], BF16, align_bytes=64)
+            vector_cols = HEAD_VECTOR_COLS if t == 0 else 0
+            if vector_cols > 0:
+                regroup(nc.vector.tensor_copy, grouped, raw[t, g], 0, vector_cols)
+            regroup(nc.scalar.copy, grouped, raw[t, g], vector_cols, N_TILE)
+            x_codes[t, g] = mx_pool.tile([P, N_TILE], U32, name="x_codes", align_bytes=64)
+            x_planes[t, g] = mx_pool.tile([P, N_TILE], U8, name="x_planes", align_bytes=64)
+            nc.vector.quantize_mx(
+                out=x_codes[t, g][:].bitcast(FP8X4),
+                scales=x_planes[t, g][:],
+                in_=grouped[:].rearrange("p n j -> p (n j)"),
+            )
+
+        def multiply_and_pool(t, members):
+            acc = {}
+            for m in members:
+                acc[m] = psum.tile([P, N_TILE], F32, name="acc")
+            for g in range(PASSES):
+                for m in members:
+                    nc.tensor.matmul_mx(
+                        out=acc[m][:],
+                        lhsT=w_words[:, g, 2 * P * m : 2 * P * (m + 1)].bitcast(FP4X4),
+                        lhsT_scale=w_planes[:, g, P * m : P * (m + 1)],
+                        rhs=x_codes[t, g][:].bitcast(FP8X4),
+                        rhs_scale=x_planes[t, g][:],
+                        start=(g == 0),
+                        stop=(g == PASSES - 1),
+                    )
+            for m in members:
+                pooled = pooled_pool.tile([P, TILE_IMAGE_ROWS // 2, IMAGE_COLS // 2], F32)
+                nc.vector.tensor_reduce(
+                    out=pooled[:],
+                    in_=acc[m][:].rearrange(
+                        "p (i di j dj) -> p i j di dj", di=2, j=IMAGE_COLS // 2, dj=2
+                    ),
+                    axis=mybir.AxisListType.XY,
+                    op=mybir.AluOpType.max,
+                )
+                nc.sync.dma_start(
+                    out=out_blocks[m][:, t * POOLED : (t + 1) * POOLED],
+                    in_=pooled[:].rearrange("p i j -> p (i j)"),
+                )
+
+        for g in range(PASSES):
+            quantise_chunk(0, g)
+        for t in range(COLUMN_TILES):
+            if t + 1 < COLUMN_TILES:
+                for g in range(PASSES):
+                    quantise_chunk(t + 1, g)
+            for first in range(0, ROW_TILES, GROUP):
+                multiply_and_pool(t, range(first, first + GROUP))

@@ -27,7 +27,7 @@ COLUMN_TILES = PIXELS // N_TILE
 TILE_IMAGE_ROWS = N_TILE // IMAGE_COLS
 POOLED = N_TILE // 4
 PSUM_BANKS = 8
-GROUP = 5
+GROUP = PSUM_BANKS
 HEAD_VECTOR_COLS = 352
 
 FLOPS = 2 * OUT_ROWS * CHANNELS * PIXELS
@@ -47,7 +47,7 @@ def tile_selfattentionconv2d_pa_kernel(tc, imgs, w_kv_words, w_kv_scales, out_0,
         raw_pool = ctx.enter_context(tc.tile_pool(name="raw", bufs=PASSES * COLUMN_TILES))
         grouped_pool = ctx.enter_context(tc.tile_pool(name="grouped", bufs=4))
         mx_pool = ctx.enter_context(tc.tile_pool(name="mx", bufs=PASSES * COLUMN_TILES))
-        pooled_pool = ctx.enter_context(tc.tile_pool(name="pooled", bufs=2 * GROUP))
+        pooled_pool = ctx.enter_context(tc.tile_pool(name="pooled", bufs=ROW_TILES))
         psum = ctx.enter_context(tc.psum_pool(name="psum", bufs=PSUM_BANKS))
 
         w_words = keep.tile([P, PASSES, 2 * OUT_ROWS], U8, align_bytes=64)
@@ -62,12 +62,11 @@ def tile_selfattentionconv2d_pa_kernel(tc, imgs, w_kv_words, w_kv_scales, out_0,
 
         def load_scales():
             rows = w_kv_scales.rearrange("g q n -> q g n")
-            for b in range(2):
-                for r in range(4):
-                    nc.sync.dma_start(
-                        out=w_planes[32 * b + r : P : 64].bitcast(I32),
-                        in_=rows[4 * b + r : 16 : 8].bitcast(I32),
-                    )
+            for r in range(4):
+                nc.sync.dma_start(
+                    out=w_planes[r : P : 32].bitcast(I32),
+                    in_=rows[r : 16 : 4].bitcast(I32),
+                )
 
         def load_words(g):
             nc.sync.dma_start(out=w_words[:, g, :].bitcast(I32), in_=w_kv_words[g].bitcast(I32))
@@ -142,4 +141,4 @@ def tile_selfattentionconv2d_pa_kernel(tc, imgs, w_kv_words, w_kv_scales, out_0,
                 for g in range(PASSES):
                     quantise_chunk(t + 1, g)
             for first in range(0, ROW_TILES, GROUP):
-                multiply_and_pool(t, range(first, first + GROUP))
+                multiply_and_pool(t, range(first, min(first + GROUP, ROW_TILES)))

@@ -27,7 +27,8 @@ COLUMN_TILES = PIXELS // N_TILE
 TILE_IMAGE_ROWS = N_TILE // IMAGE_COLS
 POOLED = N_TILE // 4
 PSUM_BANKS = 8
-GROUP = PSUM_BANKS
+HEAD_GROUP = PSUM_BANKS
+GROUP = PSUM_BANKS - 2
 HEAD_VECTOR_COLS = 352
 
 FLOPS = 2 * OUT_ROWS * CHANNELS * PIXELS
@@ -72,8 +73,8 @@ def tile_selfattentionconv2d_pa_kernel(tc, imgs, w_kv_words, w_kv_scales, out_0,
             nc.sync.dma_start(out=w_words[:, g, :].bitcast(I32), in_=w_kv_words[g].bitcast(I32))
 
         load_chunk(0, 0)
-        load_scales()
         load_words(0)
+        load_scales()
         for g in range(1, PASSES):
             load_chunk(0, g)
             load_words(g)
@@ -140,5 +141,7 @@ def tile_selfattentionconv2d_pa_kernel(tc, imgs, w_kv_words, w_kv_scales, out_0,
             if t + 1 < COLUMN_TILES:
                 for g in range(PASSES):
                     quantise_chunk(t + 1, g)
-            for first in range(0, ROW_TILES, GROUP):
-                multiply_and_pool(t, range(first, min(first + GROUP, ROW_TILES)))
+            group = HEAD_GROUP if t == 0 else GROUP
+            multiply_and_pool(t, range(group))
+            for m in range(group, ROW_TILES):
+                multiply_and_pool(t, range(m, m + 1))

@@ -48,7 +48,7 @@ def tile_selfattentionconv2d_pa_kernel(tc, imgs, w_kv_words, w_kv_scales, out_0,
         raw_pool = ctx.enter_context(tc.tile_pool(name="raw", bufs=PASSES * COLUMN_TILES))
         grouped_pool = ctx.enter_context(tc.tile_pool(name="grouped", bufs=4))
         mx_pool = ctx.enter_context(tc.tile_pool(name="mx", bufs=PASSES * COLUMN_TILES))
-        pooled_pool = ctx.enter_context(tc.tile_pool(name="pooled", bufs=ROW_TILES))
+        pooled_pool = ctx.enter_context(tc.tile_pool(name="pooled", bufs=ROW_TILES * COLUMN_TILES))
         psum = ctx.enter_context(tc.psum_pool(name="psum", bufs=PSUM_BANKS))
 
         w_words = keep.tile([P, PASSES, 2 * OUT_ROWS], U8, align_bytes=64)

@@ -30,6 +30,7 @@ PSUM_BANKS = 8
 HEAD_GROUP = PSUM_BANKS
 GROUP = PSUM_BANKS - 2
 HEAD_VECTOR_COLS = 352
+WARM_UP_MATMULS = 12
 
 FLOPS = 2 * OUT_ROWS * CHANNELS * PIXELS
 
@@ -54,6 +55,12 @@ def tile_selfattentionconv2d_pa_kernel(tc, imgs, w_kv_words, w_kv_scales, out_0,
         w_words = keep.tile([P, PASSES, 2 * OUT_ROWS], U8, align_bytes=64)
         w_planes = keep.tile([P, PASSES, OUT_ROWS], U8, align_bytes=64)
         nc.vector.memset(w_planes[:].bitcast(I32), 0)
+
+        zeros = keep.tile([P, N_TILE], BF16)
+        nc.gpsimd.memset(zeros[:], 0.0)
+        idle_sum = psum.tile([P, N_TILE], F32, name="acc")
+        for i in range(WARM_UP_MATMULS):
+            nc.tensor.matmul(out=idle_sum[:], lhsT=zeros[:, :P], rhs=zeros[:], start=True, stop=True)
 
         raw = {}
 

@@ -30,7 +30,9 @@ PSUM_BANKS = 8
 HEAD_GROUP = PSUM_BANKS
 GROUP = PSUM_BANKS - 2
 HEAD_VECTOR_COLS = 352
-WARM_UP_MATMULS = 12
+WARM_UP_MATMULS = 8
+FIRST_PIECES = 2
+SCALE_RUN = 2
 
 FLOPS = 2 * OUT_ROWS * CHANNELS * PIXELS
 
@@ -52,9 +54,11 @@ def tile_selfattentionconv2d_pa_kernel(tc, imgs, w_kv_words, w_kv_scales, out_0,
         pooled_pool = ctx.enter_context(tc.tile_pool(name="pooled", bufs=ROW_TILES * COLUMN_TILES))
         psum = ctx.enter_context(tc.psum_pool(name="psum", bufs=PSUM_BANKS))
 
-        w_words = keep.tile([P, PASSES, 2 * OUT_ROWS], U8, align_bytes=64)
+        w_words = keep.tile([P, PASSES, 2 * P * HEAD_GROUP], U8, align_bytes=64)
+        w_words_late = keep.tile([P, PASSES, 2 * P * (ROW_TILES - HEAD_GROUP)], U8, align_bytes=64)
         w_planes = keep.tile([P, PASSES, OUT_ROWS], U8, align_bytes=64)
-        nc.vector.memset(w_planes[:].bitcast(I32), 0)
+        for g in range(0, PASSES, SCALE_RUN):
+            nc.vector.memset(w_planes[:, g : g + SCALE_RUN, :].bitcast(I32), 0)
 
         zeros = keep.tile([P, N_TILE], BF16)
         nc.gpsimd.memset(zeros[:], 0.0)
@@ -64,27 +68,46 @@ def tile_selfattentionconv2d_pa_kernel(tc, imgs, w_kv_words, w_kv_scales, out_0,
 
         raw = {}
 
-        def load_chunk(t, g):
-            raw[t, g] = raw_pool.tile([P, PACK, N_TILE], BF16, name="raw")
-            nc.sync.dma_start(out=raw[t, g][:], in_=x[g][:, :, t * N_TILE : (t + 1) * N_TILE])
+        def load_chunk(t, g, pieces=1):
+            width = N_TILE // pieces
+            raw[t, g] = []
+            for first in range(t * N_TILE, (t + 1) * N_TILE, width):
+                piece = raw_pool.tile([P, PACK, width], BF16, name="raw_%d" % pieces)
+                nc.sync.dma_start(out=piece[:], in_=x[g][:, :, first : first + width])
+                raw[t, g].append(piece)
 
-        def load_scales():
+        def load_scales(g):
             rows = w_kv_scales.rearrange("g q n -> q g n")
             for r in range(4):
                 nc.sync.dma_start(
-                    out=w_planes[r : P : 32].bitcast(I32),
-                    in_=rows[r : 16 : 4].bitcast(I32),
+                    out=w_planes[r : P : 32, g : g + SCALE_RUN, :].bitcast(I32),
+                    in_=rows[r : 16 : 4, g : g + SCALE_RUN, :].bitcast(I32),
                 )
 
-        def load_words(g):
-            nc.sync.dma_start(out=w_words[:, g, :].bitcast(I32), in_=w_kv_words[g].bitcast(I32))
+        head_bytes = 2 * P * HEAD_GROUP
 
-        load_chunk(0, 0)
-        load_words(0)
-        load_scales()
-        for g in range(1, PASSES):
-            load_chunk(0, g)
+        def load_words(g):
+            nc.sync.dma_start(
+                out=w_words[:, g, :].bitcast(I32), in_=w_kv_words[g][:, :head_bytes].bitcast(I32)
+            )
+
+        def load_late_words():
+            nc.sync.dma_start(
+                out=w_words_late[:].bitcast(I32),
+                in_=w_kv_words.rearrange("g p n -> p g n")[:, :, head_bytes:].bitcast(I32),
+            )
+
+        def words_of(g, m):
+            if m < HEAD_GROUP:
+                return w_words[:, g, 2 * P * m : 2 * P * (m + 1)]
+            return w_words_late[:, g, 2 * P * (m - HEAD_GROUP) : 2 * P * (m - HEAD_GROUP + 1)]
+
+        for g in range(PASSES):
+            load_chunk(0, g, FIRST_PIECES if g == 0 else 1)
             load_words(g)
+            if g % SCALE_RUN == 0:
+                load_scales(g)
+        load_late_words()
         for t in range(1, COLUMN_TILES):
             for g in range(PASSES):
                 load_chunk(t, g)
@@ -92,25 +115,30 @@ def tile_selfattentionconv2d_pa_kernel(tc, imgs, w_kv_words, w_kv_scales, out_0,
         x_codes = {}
         x_planes = {}
 
-        def regroup(engine_copy, grouped, chunk, first, last):
+        def regroup(engine_copy, grouped, piece, first, last):
             engine_copy(
                 out=grouped[:, first:last, :].rearrange("p (c i) j -> p c j i", i=4),
-                in_=chunk[:, :, first:last].rearrange("p j (c i) -> p c j i", i=4),
+                in_=piece[:, :, first:last].rearrange("p j (c i) -> p c j i", i=4),
             )
 
         def quantise_chunk(t, g):
             grouped = grouped_pool.tile([P, N_TILE, PACK], BF16, align_bytes=64)
-            vector_cols = HEAD_VECTOR_COLS if t == 0 else 0
-            if vector_cols > 0:
-                regroup(nc.vector.tensor_copy, grouped, raw[t, g], 0, vector_cols)
-            regroup(nc.scalar.copy, grouped, raw[t, g], vector_cols, N_TILE)
             x_codes[t, g] = mx_pool.tile([P, N_TILE], U32, name="x_codes", align_bytes=64)
             x_planes[t, g] = mx_pool.tile([P, N_TILE], U8, name="x_planes", align_bytes=64)
-            nc.vector.quantize_mx(
-                out=x_codes[t, g][:].bitcast(FP8X4),
-                scales=x_planes[t, g][:],
-                in_=grouped[:].rearrange("p n j -> p (n j)"),
-            )
+            pieces = len(raw[t, g])
+            width = N_TILE // pieces
+            vector_cols = HEAD_VECTOR_COLS // pieces if t == 0 else 0
+            for i, piece in enumerate(raw[t, g]):
+                part = grouped[:, i * width : (i + 1) * width, :]
+                if vector_cols > 0:
+                    regroup(nc.vector.tensor_copy, part, piece, 0, vector_cols)
+                regroup(nc.scalar.copy, part, piece, vector_cols, width)
+            for i in range(pieces):
+                nc.vector.quantize_mx(
+                    out=x_codes[t, g][:, i * width : (i + 1) * width].bitcast(FP8X4),
+                    scales=x_planes[t, g][:, i * width : (i + 1) * width],
+                    in_=grouped[:, i * width : (i + 1) * width, :].rearrange("p n j -> p (n j)"),
+                )
 
         def multiply_and_pool(t, members):
             acc = {}
@@ -120,7 +148,7 @@ def tile_selfattentionconv2d_pa_kernel(tc, imgs, w_kv_words, w_kv_scales, out_0,
                 for m in members:
                     nc.tensor.matmul_mx(
                         out=acc[m][:],
-                        lhsT=w_words[:, g, 2 * P * m : 2 * P * (m + 1)].bitcast(FP4X4),
+                        lhsT=words_of(g, m).bitcast(FP4X4),
                         lhsT_scale=w_planes[:, g, P * m : P * (m + 1)],
                         rhs=x_codes[t, g][:].bitcast(FP8X4),
                         rhs_scale=x_planes[t, g][:],

@@ -30,7 +30,7 @@ PSUM_BANKS = 8
 HEAD_GROUP = PSUM_BANKS
 GROUP = PSUM_BANKS - 2
 HEAD_VECTOR_COLS = 352
-WARM_UP_MATMULS = 8
+WARM_UP_MATMULS = 0
 FIRST_PIECES = 2
 SCALE_RUN = 2
 

@@ -31,6 +31,7 @@ HEAD_GROUP = PSUM_BANKS
 GROUP = PSUM_BANKS - 2
 HEAD_VECTOR_COLS = 352
 WARM_UP_MATMULS = 0
+FIRST_POOLS = 3
 FIRST_PIECES = 2
 SCALE_RUN = 2
 
@@ -53,12 +54,15 @@ def tile_selfattentionconv2d_pa_kernel(tc, imgs, w_kv_words, w_kv_scales, out_0,
         mx_pool = ctx.enter_context(tc.tile_pool(name="mx", bufs=PASSES * COLUMN_TILES))
         pooled_pool = ctx.enter_context(tc.tile_pool(name="pooled", bufs=ROW_TILES * COLUMN_TILES))
         psum = ctx.enter_context(tc.psum_pool(name="psum", bufs=PSUM_BANKS))
+        ctx.enter_context(tc.manual_schedule())
 
         w_words = keep.tile([P, PASSES, 2 * P * HEAD_GROUP], U8, align_bytes=64)
         w_words_late = keep.tile([P, PASSES, 2 * P * (ROW_TILES - HEAD_GROUP)], U8, align_bytes=64)
-        w_planes = keep.tile([P, PASSES, OUT_ROWS], U8, align_bytes=64)
+        w_planes = keep.tile([P, PASSES, P * HEAD_GROUP], U8, align_bytes=64)
+        w_planes_late = keep.tile([P, PASSES, P * (ROW_TILES - HEAD_GROUP)], U8, align_bytes=64)
         for g in range(0, PASSES, SCALE_RUN):
             nc.vector.memset(w_planes[:, g : g + SCALE_RUN, :].bitcast(I32), 0)
+        nc.gpsimd.memset(w_planes_late[:].bitcast(I32), 0)
 
         zeros = keep.tile([P, N_TILE], BF16)
         nc.gpsimd.memset(zeros[:], 0.0)
@@ -81,7 +85,15 @@ def tile_selfattentionconv2d_pa_kernel(tc, imgs, w_kv_words, w_kv_scales, out_0,
             for r in range(4):
                 nc.sync.dma_start(
                     out=w_planes[r : P : 32, g : g + SCALE_RUN, :].bitcast(I32),
-                    in_=rows[r : 16 : 4, g : g + SCALE_RUN, :].bitcast(I32),
+                    in_=rows[r : 16 : 4, g : g + SCALE_RUN, : P * HEAD_GROUP].bitcast(I32),
+                )
+
+        def load_late_scales():
+            rows = w_kv_scales.rearrange("g q n -> q g n")
+            for r in range(4):
+                nc.sync.dma_start(
+                    out=w_planes_late[r : P : 32, :, :].bitcast(I32),
+                    in_=rows[r : 16 : 4, :, P * HEAD_GROUP :].bitcast(I32),
                 )
 
         head_bytes = 2 * P * HEAD_GROUP
@@ -102,16 +114,24 @@ def tile_selfattentionconv2d_pa_kernel(tc, imgs, w_kv_words, w_kv_scales, out_0,
                 return w_words[:, g, 2 * P * m : 2 * P * (m + 1)]
             return w_words_late[:, g, 2 * P * (m - HEAD_GROUP) : 2 * P * (m - HEAD_GROUP + 1)]
 
+        def scales_of(g, m):
+            if m < HEAD_GROUP:
+                return w_planes[:, g, P * m : P * (m + 1)]
+            return w_planes_late[:, g, P * (m - HEAD_GROUP) : P * (m - HEAD_GROUP + 1)]
+
         for g in range(PASSES):
             load_chunk(0, g, FIRST_PIECES if g == 0 else 1)
             load_words(g)
             if g % SCALE_RUN == 0:
                 load_scales(g)
-        load_late_words()
         for t in range(1, COLUMN_TILES):
             for g in range(PASSES):
                 load_chunk(t, g)
+                if t == 1 and g == 0:
+                    load_late_words()
+                    load_late_scales()
 
+        grouped = {}
         x_codes = {}
         x_planes = {}
 
@@ -121,27 +141,32 @@ def tile_selfattentionconv2d_pa_kernel(tc, imgs, w_kv_words, w_kv_scales, out_0,
                 in_=piece[:, :, first:last].rearrange("p j (c i) -> p c j i", i=4),
             )
 
-        def quantise_chunk(t, g):
-            grouped = grouped_pool.tile([P, N_TILE, PACK], BF16, align_bytes=64)
-            x_codes[t, g] = mx_pool.tile([P, N_TILE], U32, name="x_codes", align_bytes=64)
-            x_planes[t, g] = mx_pool.tile([P, N_TILE], U8, name="x_planes", align_bytes=64)
+        def regroup_chunk(t, g):
+            grouped[t, g] = grouped_pool.tile([P, N_TILE, PACK], BF16, name="grouped", align_bytes=64)
             pieces = len(raw[t, g])
             width = N_TILE // pieces
             vector_cols = HEAD_VECTOR_COLS // pieces if t == 0 else 0
             for i, piece in enumerate(raw[t, g]):
-                part = grouped[:, i * width : (i + 1) * width, :]
+                part = grouped[t, g][:, i * width : (i + 1) * width, :]
                 if vector_cols > 0:
                     regroup(nc.vector.tensor_copy, part, piece, 0, vector_cols)
                 regroup(nc.scalar.copy, part, piece, vector_cols, width)
+
+        def quantise_chunk(t, g):
+            x_codes[t, g] = mx_pool.tile([P, N_TILE], U32, name="x_codes", align_bytes=64)
+            x_planes[t, g] = mx_pool.tile([P, N_TILE], U8, name="x_planes", align_bytes=64)
+            pieces = len(raw[t, g])
+            width = N_TILE // pieces
             for i in range(pieces):
                 nc.vector.quantize_mx(
                     out=x_codes[t, g][:, i * width : (i + 1) * width].bitcast(FP8X4),
                     scales=x_planes[t, g][:, i * width : (i + 1) * width],
-                    in_=grouped[:, i * width : (i + 1) * width, :].rearrange("p n j -> p (n j)"),
+                    in_=grouped[t, g][:, i * width : (i + 1) * width, :].rearrange("p n j -> p (n j)"),
                 )
 
-        def multiply_and_pool(t, members):
-            acc = {}
+        acc = {}
+
+        def multiply(t, members):
             for m in members:
                 acc[m] = psum.tile([P, N_TILE], F32, name="acc")
             for g in range(PASSES):
@@ -149,12 +174,14 @@ def tile_selfattentionconv2d_pa_kernel(tc, imgs, w_kv_words, w_kv_scales, out_0,
                     nc.tensor.matmul_mx(
                         out=acc[m][:],
                         lhsT=words_of(g, m).bitcast(FP4X4),
-                        lhsT_scale=w_planes[:, g, P * m : P * (m + 1)],
+                        lhsT_scale=scales_of(g, m),
                         rhs=x_codes[t, g][:].bitcast(FP8X4),
                         rhs_scale=x_planes[t, g][:],
                         start=(g == 0),
                         stop=(g == PASSES - 1),
                     )
+
+        def pool_rows(t, members):
             for m in members:
                 pooled = pooled_pool.tile([P, TILE_IMAGE_ROWS // 2, IMAGE_COLS // 2], F32)
                 nc.vector.tensor_reduce(
@@ -171,12 +198,25 @@ def tile_selfattentionconv2d_pa_kernel(tc, imgs, w_kv_words, w_kv_scales, out_0,
                 )
 
         for g in range(PASSES):
+            regroup_chunk(0, g)
             quantise_chunk(0, g)
         for t in range(COLUMN_TILES):
-            if t + 1 < COLUMN_TILES:
-                for g in range(PASSES):
-                    quantise_chunk(t + 1, g)
             group = HEAD_GROUP if t == 0 else GROUP
-            multiply_and_pool(t, range(group))
+            more = t + 1 < COLUMN_TILES
+            if more:
+                for g in range(PASSES):
+                    regroup_chunk(t + 1, g)
+            multiply(t, range(group))
             for m in range(group, ROW_TILES):
-                multiply_and_pool(t, range(m, m + 1))
+                multiply(t, range(m, m + 1))
+            first = FIRST_POOLS if t == 0 else GROUP
+            pool_rows(t, range(first))
+            if more:
+                quantise_chunk(t + 1, 0)
+            pool_rows(t, range(first, ROW_TILES - 2 if t == 0 else ROW_TILES - 1))
+            if more:
+                quantise_chunk(t + 1, 1)
+            pool_rows(t, range(ROW_TILES - 2 if t == 0 else ROW_TILES - 1, ROW_TILES))
+            if more:
+                quantise_chunk(t + 1, 2)
+                quantise_chunk(t + 1, 3)

@@ -30,7 +30,6 @@ PSUM_BANKS = 8
 HEAD_GROUP = PSUM_BANKS
 GROUP = PSUM_BANKS - 2
 HEAD_VECTOR_COLS = 352
-WARM_UP_MATMULS = 0
 FIRST_POOLS = 3
 FIRST_PIECES = 2
 SCALE_RUN = 2
@@ -56,19 +55,15 @@ def tile_selfattentionconv2d_pa_kernel(tc, imgs, w_kv_words, w_kv_scales, out_0,
         psum = ctx.enter_context(tc.psum_pool(name="psum", bufs=PSUM_BANKS))
         ctx.enter_context(tc.manual_schedule())
 
-        w_words = keep.tile([P, PASSES, 2 * P * HEAD_GROUP], U8, align_bytes=64)
-        w_words_late = keep.tile([P, PASSES, 2 * P * (ROW_TILES - HEAD_GROUP)], U8, align_bytes=64)
-        w_planes = keep.tile([P, PASSES, P * HEAD_GROUP], U8, align_bytes=64)
-        w_planes_late = keep.tile([P, PASSES, P * (ROW_TILES - HEAD_GROUP)], U8, align_bytes=64)
+        w_words = keep.tile([P, PASSES, 2 * P * HEAD_GROUP], U8, align_bytes=256)
+        w_words_late = keep.tile([P, PASSES, 2 * P * (ROW_TILES - HEAD_GROUP)], U8, align_bytes=256)
+        w_planes_room = keep.tile([P, 192 + PASSES * P * HEAD_GROUP], U8, align_bytes=256)
+        w_planes = w_planes_room[:, 192:].rearrange("p (g n) -> p g n", g=PASSES)
+        w_planes_late_room = keep.tile([P, 192 + PASSES * P * (ROW_TILES - HEAD_GROUP)], U8, align_bytes=256)
+        w_planes_late = w_planes_late_room[:, 192:].rearrange("p (g n) -> p g n", g=PASSES)
         for g in range(0, PASSES, SCALE_RUN):
             nc.vector.memset(w_planes[:, g : g + SCALE_RUN, :].bitcast(I32), 0)
-        nc.gpsimd.memset(w_planes_late[:].bitcast(I32), 0)
-
-        zeros = keep.tile([P, N_TILE], BF16)
-        nc.gpsimd.memset(zeros[:], 0.0)
-        idle_sum = psum.tile([P, N_TILE], F32, name="acc")
-        for i in range(WARM_UP_MATMULS):
-            nc.tensor.matmul(out=idle_sum[:], lhsT=zeros[:, :P], rhs=zeros[:], start=True, stop=True)
+        nc.gpsimd.memset(w_planes_late_room[:, 192:].bitcast(I32), 0)
 
         raw = {}
 
@@ -153,8 +148,10 @@ def tile_selfattentionconv2d_pa_kernel(tc, imgs, w_kv_words, w_kv_scales, out_0,
                 regroup(nc.scalar.copy, part, piece, vector_cols, width)
 
         def quantise_chunk(t, g):
-            x_codes[t, g] = mx_pool.tile([P, N_TILE], U32, name="x_codes", align_bytes=64)
-            x_planes[t, g] = mx_pool.tile([P, N_TILE], U8, name="x_planes", align_bytes=64)
+            codes_room = mx_pool.tile([P, 32 + N_TILE], U32, name="x_codes", align_bytes=256)
+            planes_room = mx_pool.tile([P, 64 + N_TILE], U8, name="x_planes", align_bytes=256)
+            x_codes[t, g] = codes_room[:, 32:]
+            x_planes[t, g] = planes_room[:, 64:]
             pieces = len(raw[t, g])
             width = N_TILE // pieces
             for i in range(pieces):

@@ -55,15 +55,13 @@ def tile_selfattentionconv2d_pa_kernel(tc, imgs, w_kv_words, w_kv_scales, out_0,
         psum = ctx.enter_context(tc.psum_pool(name="psum", bufs=PSUM_BANKS))
         ctx.enter_context(tc.manual_schedule())
 
-        w_words = keep.tile([P, PASSES, 2 * P * HEAD_GROUP], U8, align_bytes=256)
-        w_words_late = keep.tile([P, PASSES, 2 * P * (ROW_TILES - HEAD_GROUP)], U8, align_bytes=256)
-        w_planes_room = keep.tile([P, 192 + PASSES * P * HEAD_GROUP], U8, align_bytes=256)
-        w_planes = w_planes_room[:, 192:].rearrange("p (g n) -> p g n", g=PASSES)
-        w_planes_late_room = keep.tile([P, 192 + PASSES * P * (ROW_TILES - HEAD_GROUP)], U8, align_bytes=256)
-        w_planes_late = w_planes_late_room[:, 192:].rearrange("p (g n) -> p g n", g=PASSES)
+        w_words = keep.tile([P, 192 + PASSES * 2 * P * HEAD_GROUP], U8, align_bytes=256)
+        w_words_late = keep.tile([P, 192 + PASSES * 2 * P * (ROW_TILES - HEAD_GROUP)], U8, align_bytes=256)
+        w_planes = keep.tile([P, PASSES, P * HEAD_GROUP], U8, align_bytes=256)
+        w_planes_late = keep.tile([P, PASSES, P * (ROW_TILES - HEAD_GROUP)], U8, align_bytes=256)
         for g in range(0, PASSES, SCALE_RUN):
             nc.vector.memset(w_planes[:, g : g + SCALE_RUN, :].bitcast(I32), 0)
-        nc.gpsimd.memset(w_planes_late_room[:, 192:].bitcast(I32), 0)
+        nc.gpsimd.memset(w_planes_late[:].bitcast(I32), 0)
 
         raw = {}
 
@@ -95,19 +93,21 @@ def tile_selfattentionconv2d_pa_kernel(tc, imgs, w_kv_words, w_kv_scales, out_0,
 
         def load_words(g):
             nc.sync.dma_start(
-                out=w_words[:, g, :].bitcast(I32), in_=w_kv_words[g][:, :head_bytes].bitcast(I32)
+                out=w_words[:, 192 + g * head_bytes : 192 + (g + 1) * head_bytes].bitcast(I32), in_=w_kv_words[g][:, :head_bytes].bitcast(I32)
             )
 
         def load_late_words():
             nc.sync.dma_start(
-                out=w_words_late[:].bitcast(I32),
+                out=w_words_late[:, 192:].rearrange("p (g n) -> p g n", g=PASSES).bitcast(I32),
                 in_=w_kv_words.rearrange("g p n -> p g n")[:, :, head_bytes:].bitcast(I32),
             )
 
         def words_of(g, m):
             if m < HEAD_GROUP:
-                return w_words[:, g, 2 * P * m : 2 * P * (m + 1)]
-            return w_words_late[:, g, 2 * P * (m - HEAD_GROUP) : 2 * P * (m - HEAD_GROUP + 1)]
+                first = 192 + g * head_bytes + 2 * P * m
+                return w_words[:, first : first + 2 * P]
+            first = 192 + 2 * P * (g * (ROW_TILES - HEAD_GROUP) + m - HEAD_GROUP)
+            return w_words_late[:, first : first + 2 * P]
 
         def scales_of(g, m):
             if m < HEAD_GROUP:

@@ -32,7 +32,12 @@ GROUP = PSUM_BANKS - 2
 HEAD_VECTOR_COLS = 352
 FIRST_POOLS = 3
 FIRST_PIECES = 2
+NARROW = 128
 SCALE_RUN = 2
+
+WORDS_AT = 192
+CODES_AT = 128
+PLANES_AT = 64
 
 FLOPS = 2 * OUT_ROWS * CHANNELS * PIXELS
 
@@ -55,8 +60,8 @@ def tile_selfattentionconv2d_pa_kernel(tc, imgs, w_kv_words, w_kv_scales, out_0,
         psum = ctx.enter_context(tc.psum_pool(name="psum", bufs=PSUM_BANKS))
         ctx.enter_context(tc.manual_schedule())
 
-        w_words = keep.tile([P, 192 + PASSES * 2 * P * HEAD_GROUP], U8, align_bytes=256)
-        w_words_late = keep.tile([P, 192 + PASSES * 2 * P * (ROW_TILES - HEAD_GROUP)], U8, align_bytes=256)
+        w_words = keep.tile([P, WORDS_AT + PASSES * 2 * P * HEAD_GROUP], U8, align_bytes=256)
+        w_words_late = keep.tile([P, WORDS_AT + PASSES * 2 * P * (ROW_TILES - HEAD_GROUP)], U8, align_bytes=256)
         w_planes = keep.tile([P, PASSES, P * HEAD_GROUP], U8, align_bytes=256)
         w_planes_late = keep.tile([P, PASSES, P * (ROW_TILES - HEAD_GROUP)], U8, align_bytes=256)
         for g in range(0, PASSES, SCALE_RUN):
@@ -65,13 +70,12 @@ def tile_selfattentionconv2d_pa_kernel(tc, imgs, w_kv_words, w_kv_scales, out_0,
 
         raw = {}
 
-        def load_chunk(t, g, pieces=1):
+        def load_piece(t, g, i=0, pieces=1):
             width = N_TILE // pieces
-            raw[t, g] = []
-            for first in range(t * N_TILE, (t + 1) * N_TILE, width):
-                piece = raw_pool.tile([P, PACK, width], BF16, name="raw_%d" % pieces)
-                nc.sync.dma_start(out=piece[:], in_=x[g][:, :, first : first + width])
-                raw[t, g].append(piece)
+            first = t * N_TILE + i * width
+            piece = raw_pool.tile([P, PACK, width], BF16, name="raw_%d" % pieces)
+            nc.sync.dma_start(out=piece[:], in_=x[g][:, :, first : first + width])
+            raw.setdefault((t, g), []).append(piece)
 
         def load_scales(g):
             rows = w_kv_scales.rearrange("g q n -> q g n")
@@ -93,20 +97,20 @@ def tile_selfattentionconv2d_pa_kernel(tc, imgs, w_kv_words, w_kv_scales, out_0,
 
         def load_words(g):
             nc.sync.dma_start(
-                out=w_words[:, 192 + g * head_bytes : 192 + (g + 1) * head_bytes].bitcast(I32), in_=w_kv_words[g][:, :head_bytes].bitcast(I32)
+                out=w_words[:, WORDS_AT + g * head_bytes : WORDS_AT + (g + 1) * head_bytes].bitcast(I32), in_=w_kv_words[g][:, :head_bytes].bitcast(I32)
             )
 
         def load_late_words():
             nc.sync.dma_start(
-                out=w_words_late[:, 192:].rearrange("p (g n) -> p g n", g=PASSES).bitcast(I32),
+                out=w_words_late[:, WORDS_AT:].rearrange("p (g n) -> p g n", g=PASSES).bitcast(I32),
                 in_=w_kv_words.rearrange("g p n -> p g n")[:, :, head_bytes:].bitcast(I32),
             )
 
         def words_of(g, m):
             if m < HEAD_GROUP:
-                first = 192 + g * head_bytes + 2 * P * m
+                first = WORDS_AT + g * head_bytes + 2 * P * m
                 return w_words[:, first : first + 2 * P]
-            first = 192 + 2 * P * (g * (ROW_TILES - HEAD_GROUP) + m - HEAD_GROUP)
+            first = WORDS_AT + 2 * P * (g * (ROW_TILES - HEAD_GROUP) + m - HEAD_GROUP)
             return w_words_late[:, first : first + 2 * P]
 
         def scales_of(g, m):
@@ -114,14 +118,19 @@ def tile_selfattentionconv2d_pa_kernel(tc, imgs, w_kv_words, w_kv_scales, out_0,
                 return w_planes[:, g, P * m : P * (m + 1)]
             return w_planes_late[:, g, P * (m - HEAD_GROUP) : P * (m - HEAD_GROUP + 1)]
 
-        for g in range(PASSES):
-            load_chunk(0, g, FIRST_PIECES if g == 0 else 1)
+        load_piece(0, 0, 0, FIRST_PIECES)
+        load_words(0)
+        load_scales(0)
+        for i in range(1, FIRST_PIECES):
+            load_piece(0, 0, i, FIRST_PIECES)
+        for g in range(1, PASSES):
+            load_piece(0, g)
             load_words(g)
             if g % SCALE_RUN == 0:
                 load_scales(g)
         for t in range(1, COLUMN_TILES):
             for g in range(PASSES):
-                load_chunk(t, g)
+                load_piece(t, g)
                 if t == 1 and g == 0:
                     load_late_words()
                     load_late_scales()
@@ -136,30 +145,29 @@ def tile_selfattentionconv2d_pa_kernel(tc, imgs, w_kv_words, w_kv_scales, out_0,
                 in_=piece[:, :, first:last].rearrange("p j (c i) -> p c j i", i=4),
             )
 
-        def regroup_chunk(t, g):
-            grouped[t, g] = grouped_pool.tile([P, N_TILE, PACK], BF16, name="grouped", align_bytes=64)
+        def regroup_piece(t, g, i):
+            if i == 0:
+                grouped[t, g] = grouped_pool.tile([P, N_TILE, PACK], BF16, name="grouped", align_bytes=64)
             pieces = len(raw[t, g])
             width = N_TILE // pieces
             vector_cols = HEAD_VECTOR_COLS // pieces if t == 0 else 0
-            for i, piece in enumerate(raw[t, g]):
-                part = grouped[t, g][:, i * width : (i + 1) * width, :]
-                if vector_cols > 0:
-                    regroup(nc.vector.tensor_copy, part, piece, 0, vector_cols)
-                regroup(nc.scalar.copy, part, piece, vector_cols, width)
+            part = grouped[t, g][:, i * width : (i + 1) * width, :]
+            if vector_cols > 0:
+                regroup(nc.vector.tensor_copy, part, raw[t, g][i], 0, vector_cols)
+            regroup(nc.scalar.copy, part, raw[t, g][i], vector_cols, width)
 
-        def quantise_chunk(t, g):
-            codes_room = mx_pool.tile([P, 32 + N_TILE], U32, name="x_codes", align_bytes=256)
-            planes_room = mx_pool.tile([P, 64 + N_TILE], U8, name="x_planes", align_bytes=256)
-            x_codes[t, g] = codes_room[:, 32:]
-            x_planes[t, g] = planes_room[:, 64:]
-            pieces = len(raw[t, g])
-            width = N_TILE // pieces
-            for i in range(pieces):
-                nc.vector.quantize_mx(
-                    out=x_codes[t, g][:, i * width : (i + 1) * width].bitcast(FP8X4),
-                    scales=x_planes[t, g][:, i * width : (i + 1) * width],
-                    in_=grouped[t, g][:, i * width : (i + 1) * width, :].rearrange("p n j -> p (n j)"),
-                )
+        def quantise_piece(t, g, i):
+            if i == 0:
+                codes_room = mx_pool.tile([P, CODES_AT // 4 + N_TILE], U32, name="x_codes", align_bytes=256)
+                planes_room = mx_pool.tile([P, PLANES_AT + N_TILE], U8, name="x_planes", align_bytes=256)
+                x_codes[t, g] = codes_room[:, CODES_AT // 4 :]
+                x_planes[t, g] = planes_room[:, PLANES_AT:]
+            width = N_TILE // len(raw[t, g])
+            nc.vector.quantize_mx(
+                out=x_codes[t, g][:, i * width : (i + 1) * width].bitcast(FP8X4),
+                scales=x_planes[t, g][:, i * width : (i + 1) * width],
+                in_=grouped[t, g][:, i * width : (i + 1) * width, :].rearrange("p n j -> p (n j)"),
+            )
 
         acc = {}
 
@@ -167,16 +175,20 @@ def tile_selfattentionconv2d_pa_kernel(tc, imgs, w_kv_words, w_kv_scales, out_0,
             for m in members:
                 acc[m] = psum.tile([P, N_TILE], F32, name="acc")
             for g in range(PASSES):
-                for m in members:
-                    nc.tensor.matmul_mx(
-                        out=acc[m][:],
-                        lhsT=words_of(g, m).bitcast(FP4X4),
-                        lhsT_scale=scales_of(g, m),
-                        rhs=x_codes[t, g][:].bitcast(FP8X4),
-                        rhs_scale=x_planes[t, g][:],
-                        start=(g == 0),
-                        stop=(g == PASSES - 1),
-                    )
+                width = N_TILE if len(raw[t, g]) == 1 or len(members) == 1 else NARROW
+                pieces = len(raw[t, g]) if width == NARROW else 1
+                for i in range(pieces):
+                    for m in members:
+                        for first in range(i * N_TILE // pieces, (i + 1) * N_TILE // pieces, width):
+                            nc.tensor.matmul_mx(
+                                out=acc[m][:, first : first + width],
+                                lhsT=words_of(g, m).bitcast(FP4X4),
+                                lhsT_scale=scales_of(g, m),
+                                rhs=x_codes[t, g][:, first : first + width].bitcast(FP8X4),
+                                rhs_scale=x_planes[t, g][:, first : first + width],
+                                start=(g == 0 and first == 0),
+                                stop=(g == PASSES - 1),
+                            )
 
         def pool_rows(t, members):
             for m in members:
@@ -194,26 +206,66 @@ def tile_selfattentionconv2d_pa_kernel(tc, imgs, w_kv_words, w_kv_scales, out_0,
                     in_=pooled[:].rearrange("p i j -> p (i j)"),
                 )
 
+        parts = []
+
+        def multiply_in_parts(t, m):
+            for first in range(0, N_TILE, NARROW):
+                part = psum.tile([P, N_TILE], F32, name="acc")
+                for g in range(PASSES):
+                    nc.tensor.matmul_mx(
+                        out=part[:, :NARROW],
+                        lhsT=words_of(g, m).bitcast(FP4X4),
+                        lhsT_scale=scales_of(g, m),
+                        rhs=x_codes[t, g][:, first : first + NARROW].bitcast(FP8X4),
+                        rhs_scale=x_planes[t, g][:, first : first + NARROW],
+                        start=(g == 0),
+                        stop=(g == PASSES - 1),
+                    )
+                parts.append(part)
+
+        def pool_parts(t, m):
+            pooled = pooled_pool.tile([P, TILE_IMAGE_ROWS // 2, IMAGE_COLS // 2], F32)
+            rows = TILE_IMAGE_ROWS // 2 // len(parts)
+            for i, part in enumerate(parts):
+                nc.vector.tensor_reduce(
+                    out=pooled[:, i * rows : (i + 1) * rows, :],
+                    in_=part[:, :NARROW].rearrange(
+                        "p (i di j dj) -> p i j di dj", di=2, j=IMAGE_COLS // 2, dj=2
+                    ),
+                    axis=mybir.AxisListType.XY,
+                    op=mybir.AluOpType.max,
+                )
+            nc.sync.dma_start(
+                out=out_blocks[m][:, t * POOLED : (t + 1) * POOLED],
+                in_=pooled[:].rearrange("p i j -> p (i j)"),
+            )
+
         for g in range(PASSES):
-            regroup_chunk(0, g)
-            quantise_chunk(0, g)
+            for i in range(len(raw[0, g])):
+                regroup_piece(0, g, i)
+                quantise_piece(0, g, i)
         for t in range(COLUMN_TILES):
             group = HEAD_GROUP if t == 0 else GROUP
             more = t + 1 < COLUMN_TILES
             if more:
                 for g in range(PASSES):
-                    regroup_chunk(t + 1, g)
+                    regroup_piece(t + 1, g, 0)
             multiply(t, range(group))
             for m in range(group, ROW_TILES):
-                multiply(t, range(m, m + 1))
+                if more or m < ROW_TILES - 1:
+                    multiply(t, range(m, m + 1))
+                else:
+                    multiply_in_parts(t, m)
             first = FIRST_POOLS if t == 0 else GROUP
             pool_rows(t, range(first))
             if more:
-                quantise_chunk(t + 1, 0)
+                quantise_piece(t + 1, 0, 0)
             pool_rows(t, range(first, ROW_TILES - 2 if t == 0 else ROW_TILES - 1))
             if more:
-                quantise_chunk(t + 1, 1)
-            pool_rows(t, range(ROW_TILES - 2 if t == 0 else ROW_TILES - 1, ROW_TILES))
+                quantise_piece(t + 1, 1, 0)
             if more:
-                quantise_chunk(t + 1, 2)
-                quantise_chunk(t + 1, 3)
+                pool_rows(t, range(ROW_TILES - 2 if t == 0 else ROW_TILES - 1, ROW_TILES))
+                quantise_piece(t + 1, 2, 0)
+                quantise_piece(t + 1, 3, 0)
+            else:
+                pool_parts(t, ROW_TILES - 1)

@@ -27,6 +27,7 @@ COLUMN_TILES = PIXELS // N_TILE
 TILE_IMAGE_ROWS = N_TILE // IMAGE_COLS
 POOLED = N_TILE // 4
 PSUM_BANKS = 8
+BANK_BYTES = 2048
 HEAD_GROUP = PSUM_BANKS
 GROUP = PSUM_BANKS - 2
 HEAD_VECTOR_COLS = 352
@@ -57,7 +58,7 @@ def tile_selfattentionconv2d_pa_kernel(tc, imgs, w_kv_words, w_kv_scales, out_0,
         grouped_pool = ctx.enter_context(tc.tile_pool(name="grouped", bufs=4))
         mx_pool = ctx.enter_context(tc.tile_pool(name="mx", bufs=PASSES * COLUMN_TILES))
         pooled_pool = ctx.enter_context(tc.tile_pool(name="pooled", bufs=ROW_TILES * COLUMN_TILES))
-        psum = ctx.enter_context(tc.psum_pool(name="psum", bufs=PSUM_BANKS))
+        psum = ctx.enter_context(tc.psum_pool(name="psum", bufs=1))
         ctx.enter_context(tc.manual_schedule())
 
         w_words = keep.tile([P, WORDS_AT + PASSES * 2 * P * HEAD_GROUP], U8, align_bytes=256)
@@ -170,10 +171,17 @@ def tile_selfattentionconv2d_pa_kernel(tc, imgs, w_kv_words, w_kv_scales, out_0,
             )
 
         acc = {}
+        banks_used = []
+
+        def next_bank():
+            turn = len(banks_used) % PSUM_BANKS
+            bank = (turn % 2) * (PSUM_BANKS // 2) + turn // 2
+            banks_used.append(bank)
+            return psum.tile([P, N_TILE], F32, name="bank_%d" % bank, offset=bank * BANK_BYTES)
 
         def multiply(t, members):
             for m in members:
-                acc[m] = psum.tile([P, N_TILE], F32, name="acc")
+                acc[m] = next_bank()
             for g in range(PASSES):
                 width = N_TILE if len(raw[t, g]) == 1 or len(members) == 1 else NARROW
                 pieces = len(raw[t, g]) if width == NARROW else 1
@@ -210,7 +218,7 @@ def tile_selfattentionconv2d_pa_kernel(tc, imgs, w_kv_words, w_kv_scales, out_0,
 
         def multiply_in_parts(t, m):
             for first in range(0, N_TILE, NARROW):
-                part = psum.tile([P, N_TILE], F32, name="acc")
+                part = next_bank()
                 for g in range(PASSES):
                     nc.tensor.matmul_mx(
                         out=part[:, :NARROW],

from contextlib import ExitStack

import concourse.mybir as mybir

BF16 = mybir.dt.bfloat16
F32 = mybir.dt.float32
I32 = mybir.dt.int32
U32 = mybir.dt.uint32
U8 = mybir.dt.uint8
FP8X4 = mybir.dt.float8_e4m3fn_x4
FP4X4 = mybir.dt.float4_e2m1fn_x4

P = 128
PACK = 4
K_PASS = P * PACK
CHANNELS = 2048
IMAGE_ROWS = 64
IMAGE_COLS = 32
PIXELS = IMAGE_ROWS * IMAGE_COLS
KEY_ROWS = 256
VALUE_ROWS = 1024
OUT_ROWS = KEY_ROWS + VALUE_ROWS
PASSES = CHANNELS // K_PASS
ROW_TILES = OUT_ROWS // P
N_TILE = 512
COLUMN_TILES = PIXELS // N_TILE
TILE_IMAGE_ROWS = N_TILE // IMAGE_COLS
POOLED = N_TILE // 4
PSUM_BANKS = 8
BANK_BYTES = 2048
HEAD_GROUP = PSUM_BANKS
GROUP = PSUM_BANKS - 2
HEAD_VECTOR_COLS = 352
FIRST_POOLS = 3
FIRST_PIECES = 2
NARROW = 128
SCALE_RUN = 2

WORDS_AT = 192
CODES_AT = 128
PLANES_AT = 64

FLOPS = 2 * OUT_ROWS * CHANNELS * PIXELS


def tile_selfattentionconv2d_pa_kernel(tc, imgs, w_kv_words, w_kv_scales, out_0, out_1):
    nc = tc.nc

    x = imgs.rearrange("b (g p j) h w -> (b g) p j (h w)", p=P, j=PACK)
    key_blocks = out_0.rearrange("b (m p) i j -> (b m) p (i j)", p=P)
    value_blocks = out_1.rearrange("b (m p) i j -> (b m) p (i j)", p=P)
    out_blocks = [key_blocks[m] for m in range(KEY_ROWS // P)]
    out_blocks.extend([value_blocks[m] for m in range(VALUE_ROWS // P)])

    with ExitStack() as ctx:
        keep = ctx.enter_context(tc.tile_pool(name="keep", bufs=1))
        raw_pool = ctx.enter_context(tc.tile_pool(name="raw", bufs=PASSES * COLUMN_TILES))
        grouped_pool = ctx.enter_context(tc.tile_pool(name="grouped", bufs=4))
        mx_pool = ctx.enter_context(tc.tile_pool(name="mx", bufs=PASSES * COLUMN_TILES))
        pooled_pool = ctx.enter_context(tc.tile_pool(name="pooled", bufs=ROW_TILES * COLUMN_TILES))
        psum = ctx.enter_context(tc.psum_pool(name="psum", bufs=1))
        ctx.enter_context(tc.manual_schedule())

        w_words = keep.tile([P, WORDS_AT + PASSES * 2 * P * HEAD_GROUP], U8, align_bytes=256)
        w_words_late = keep.tile([P, WORDS_AT + PASSES * 2 * P * (ROW_TILES - HEAD_GROUP)], U8, align_bytes=256)
        w_planes = keep.tile([P, PASSES, P * HEAD_GROUP], U8, align_bytes=256)
        w_planes_late = keep.tile([P, PASSES, P * (ROW_TILES - HEAD_GROUP)], U8, align_bytes=256)
        for g in range(0, PASSES, SCALE_RUN):
            nc.vector.memset(w_planes[:, g : g + SCALE_RUN, :].bitcast(I32), 0)
        nc.gpsimd.memset(w_planes_late[:].bitcast(I32), 0)

        raw = {}

        def load_piece(t, g, i=0, pieces=1):
            width = N_TILE // pieces
            first = t * N_TILE + i * width
            piece = raw_pool.tile([P, PACK, width], BF16, name="raw_%d" % pieces)
            nc.sync.dma_start(out=piece[:], in_=x[g][:, :, first : first + width])
            raw.setdefault((t, g), []).append(piece)

        def load_scales(g):
            rows = w_kv_scales.rearrange("g q n -> q g n")
            for r in range(4):
                nc.sync.dma_start(
                    out=w_planes[r : P : 32, g : g + SCALE_RUN, :].bitcast(I32),
                    in_=rows[r : 16 : 4, g : g + SCALE_RUN, : P * HEAD_GROUP].bitcast(I32),
                )

        def load_late_scales():
            rows = w_kv_scales.rearrange("g q n -> q g n")
            for r in range(4):
                nc.sync.dma_start(
                    out=w_planes_late[r : P : 32, :, :].bitcast(I32),
                    in_=rows[r : 16 : 4, :, P * HEAD_GROUP :].bitcast(I32),
                )

        head_bytes = 2 * P * HEAD_GROUP

        def load_words(g):
            nc.sync.dma_start(
                out=w_words[:, WORDS_AT + g * head_bytes : WORDS_AT + (g + 1) * head_bytes].bitcast(I32), in_=w_kv_words[g][:, :head_bytes].bitcast(I32)
            )

        def load_late_words():
            nc.sync.dma_start(
                out=w_words_late[:, WORDS_AT:].rearrange("p (g n) -> p g n", g=PASSES).bitcast(I32),
                in_=w_kv_words.rearrange("g p n -> p g n")[:, :, head_bytes:].bitcast(I32),
            )

        def words_of(g, m):
            if m < HEAD_GROUP:
                first = WORDS_AT + g * head_bytes + 2 * P * m
                return w_words[:, first : first + 2 * P]
            first = WORDS_AT + 2 * P * (g * (ROW_TILES - HEAD_GROUP) + m - HEAD_GROUP)
            return w_words_late[:, first : first + 2 * P]

        def scales_of(g, m):
            if m < HEAD_GROUP:
                return w_planes[:, g, P * m : P * (m + 1)]
            return w_planes_late[:, g, P * (m - HEAD_GROUP) : P * (m - HEAD_GROUP + 1)]

        load_piece(0, 0, 0, FIRST_PIECES)
        load_words(0)
        load_scales(0)
        for i in range(1, FIRST_PIECES):
            load_piece(0, 0, i, FIRST_PIECES)
        for g in range(1, PASSES):
            load_piece(0, g)
            load_words(g)
            if g % SCALE_RUN == 0:
                load_scales(g)
        for t in range(1, COLUMN_TILES):
            for g in range(PASSES):
                load_piece(t, g)
                if t == 1 and g == 0:
                    load_late_words()
                    load_late_scales()

        grouped = {}
        x_codes = {}
        x_planes = {}

        def regroup(engine_copy, grouped, piece, first, last):
            engine_copy(
                out=grouped[:, first:last, :].rearrange("p (c i) j -> p c j i", i=4),
                in_=piece[:, :, first:last].rearrange("p j (c i) -> p c j i", i=4),
            )

        def regroup_piece(t, g, i):
            if i == 0:
                grouped[t, g] = grouped_pool.tile([P, N_TILE, PACK], BF16, name="grouped", align_bytes=64)
            pieces = len(raw[t, g])
            width = N_TILE // pieces
            vector_cols = HEAD_VECTOR_COLS // pieces if t == 0 else 0
            part = grouped[t, g][:, i * width : (i + 1) * width, :]
            if vector_cols > 0:
                regroup(nc.vector.tensor_copy, part, raw[t, g][i], 0, vector_cols)
            regroup(nc.scalar.copy, part, raw[t, g][i], vector_cols, width)

        def quantise_piece(t, g, i):
            if i == 0:
                codes_room = mx_pool.tile([P, CODES_AT // 4 + N_TILE], U32, name="x_codes", align_bytes=256)
                planes_room = mx_pool.tile([P, PLANES_AT + N_TILE], U8, name="x_planes", align_bytes=256)
                x_codes[t, g] = codes_room[:, CODES_AT // 4 :]
                x_planes[t, g] = planes_room[:, PLANES_AT:]
            width = N_TILE // len(raw[t, g])
            nc.vector.quantize_mx(
                out=x_codes[t, g][:, i * width : (i + 1) * width].bitcast(FP8X4),
                scales=x_planes[t, g][:, i * width : (i + 1) * width],
                in_=grouped[t, g][:, i * width : (i + 1) * width, :].rearrange("p n j -> p (n j)"),
            )

        acc = {}
        banks_used = []

        def next_bank():
            turn = len(banks_used) % PSUM_BANKS
            bank = (turn % 2) * (PSUM_BANKS // 2) + turn // 2
            banks_used.append(bank)
            return psum.tile([P, N_TILE], F32, name="bank_%d" % bank, offset=bank * BANK_BYTES)

        def multiply(t, members):
            for m in members:
                acc[m] = next_bank()
            for g in range(PASSES):
                width = N_TILE if len(raw[t, g]) == 1 or len(members) == 1 else NARROW
                pieces = len(raw[t, g]) if width == NARROW else 1
                for i in range(pieces):
                    for m in members:
                        for first in range(i * N_TILE // pieces, (i + 1) * N_TILE // pieces, width):
                            nc.tensor.matmul_mx(
                                out=acc[m][:, first : first + width],
                                lhsT=words_of(g, m).bitcast(FP4X4),
                                lhsT_scale=scales_of(g, m),
                                rhs=x_codes[t, g][:, first : first + width].bitcast(FP8X4),
                                rhs_scale=x_planes[t, g][:, first : first + width],
                                start=(g == 0 and first == 0),
                                stop=(g == PASSES - 1),
                            )

        def pool_rows(t, members):
            for m in members:
                pooled = pooled_pool.tile([P, TILE_IMAGE_ROWS // 2, IMAGE_COLS // 2], F32)
                nc.vector.tensor_reduce(
                    out=pooled[:],
                    in_=acc[m][:].rearrange(
                        "p (i di j dj) -> p i j di dj", di=2, j=IMAGE_COLS // 2, dj=2
                    ),
                    axis=mybir.AxisListType.XY,
                    op=mybir.AluOpType.max,
                )
                nc.sync.dma_start(
                    out=out_blocks[m][:, t * POOLED : (t + 1) * POOLED],
                    in_=pooled[:].rearrange("p i j -> p (i j)"),
                )

        parts = []

        def multiply_in_parts(t, m):
            for first in range(0, N_TILE, NARROW):
                part = next_bank()
                for g in range(PASSES):
                    nc.tensor.matmul_mx(
                        out=part[:, :NARROW],
                        lhsT=words_of(g, m).bitcast(FP4X4),
                        lhsT_scale=scales_of(g, m),
                        rhs=x_codes[t, g][:, first : first + NARROW].bitcast(FP8X4),
                        rhs_scale=x_planes[t, g][:, first : first + NARROW],
                        start=(g == 0),
                        stop=(g == PASSES - 1),
                    )
                parts.append(part)

        def pool_parts(t, m):
            pooled = pooled_pool.tile([P, TILE_IMAGE_ROWS // 2, IMAGE_COLS // 2], F32)
            rows = TILE_IMAGE_ROWS // 2 // len(parts)
            for i, part in enumerate(parts):
                nc.vector.tensor_reduce(
                    out=pooled[:, i * rows : (i + 1) * rows, :],
                    in_=part[:, :NARROW].rearrange(
                        "p (i di j dj) -> p i j di dj", di=2, j=IMAGE_COLS // 2, dj=2
                    ),
                    axis=mybir.AxisListType.XY,
                    op=mybir.AluOpType.max,
                )
            nc.sync.dma_start(
                out=out_blocks[m][:, t * POOLED : (t + 1) * POOLED],
                in_=pooled[:].rearrange("p i j -> p (i j)"),
            )

        for g in range(PASSES):
            for i in range(len(raw[0, g])):
                regroup_piece(0, g, i)
                quantise_piece(0, g, i)
        for t in range(COLUMN_TILES):
            group = HEAD_GROUP if t == 0 else GROUP
            more = t + 1 < COLUMN_TILES
            if more:
                for g in range(PASSES):
                    regroup_piece(t + 1, g, 0)
            multiply(t, range(group))
            for m in range(group, ROW_TILES):
                if more or m < ROW_TILES - 1:
                    multiply(t, range(m, m + 1))
                else:
                    multiply_in_parts(t, m)
            first = FIRST_POOLS if t == 0 else GROUP
            pool_rows(t, range(first))
            if more:
                quantise_piece(t + 1, 0, 0)
            pool_rows(t, range(first, ROW_TILES - 2 if t == 0 else ROW_TILES - 1))
            if more:
                quantise_piece(t + 1, 1, 0)
            if more:
                pool_rows(t, range(ROW_TILES - 2 if t == 0 else ROW_TILES - 1, ROW_TILES))
                quantise_piece(t + 1, 2, 0)
                quantise_piece(t + 1, 3, 0)
            else:
                pool_parts(t, ROW_TILES - 1)
